import numpy as np
import ml_dtypes


def mxq(x, axis, fmt="e4m3"):
    dtype, down = {"e4m3": (ml_dtypes.float8_e4m3fn, 7), "e5m2": (ml_dtypes.float8_e5m2, 14)}[fmt]
    v = np.moveaxis(np.asarray(x, np.float32).astype(ml_dtypes.bfloat16).astype(np.float64), axis, -1)
    blocks = v.reshape(v.shape[:-1] + (-1, 32))
    amax = np.abs(blocks).max(-1, keepdims=True)
    byte = np.maximum(np.where(amax > 0, np.frexp(amax)[1] - 1 + 127, 0) - down, 1)
    scale = np.exp2(byte - 127.0)
    codes = (blocks / scale).astype(np.float32).astype(dtype).astype(np.float64)
    return np.moveaxis((codes * scale).reshape(v.shape), -1, axis)


WIDE = False


def mx_kscale(k):
    if not WIDE:
        return np.ones(k)
    levels = np.array([10, -10, 5, -5, 0])
    a = np.random.permutation(np.resize(levels, k // 512 * 4)).reshape(k // 512, 4)
    idx = np.arange(k)
    return np.exp2(a[idx // 512, idx % 128 // 32])


BF16 = ml_dtypes.bfloat16


def bf(x):
    return np.asarray(x, np.float32).astype(BF16)


def f64(x):
    return np.asarray(x).astype(np.float64)


N, E, C = 512, 4096, 512
DENSITY = 0.01


def setup_inputs():
    s, t = mx_kscale(N), mx_kscale(C)
    member = np.random.uniform(size=(N, E)) < DENSITY
    return {"node_features": bf(np.random.standard_normal((N, C)) / s[:, None] * t[None, :]),
            "incidence": bf(member * s[:, None]),
            "W1": bf(np.random.standard_normal((C, C)) * np.sqrt(E) / np.sqrt(DENSITY * N * C) / t[:, None]),
            "b1": bf(np.random.standard_normal(C) * 0.1 * np.sqrt(E)),
            "edge_attention": bf(1.0 + np.random.standard_normal(E))}


def reference(node_features, incidence, W1, b1, edge_attention):
    agg = mxq(f64(incidence), 0, "e4m3").T @ mxq(f64(node_features), 0, "e4m3")
    lin = (mxq(agg, 1, "e4m3") @ mxq(f64(W1), 0, "e4m3")) + f64(b1)
    a = f64(edge_attention)
    e = np.exp(a - a.max())
    attn = e / e.sum()
    return lin * attn[:, None]

@@ -1,0 +1,283 @@
+from contextlib import ExitStack
+
+import concourse.mybir as mybir
+from concourse.masks import make_identity
+
+F32 = mybir.dt.float32
+BF16 = mybir.dt.bfloat16
+U32 = mybir.dt.uint32
+U8 = mybir.dt.uint8
+FP8X4 = mybir.dt.float8_e4m3fn_x4
+ALU = mybir.AluOpType
+ACT = mybir.ActivationFunctionType
+AX = mybir.AxisListType
+
+P = 128
+PACK = 4
+NODES = 512
+EDGES = 4096
+CH = 512
+CHUNK = 512
+N_CHUNKS = EDGES // CHUNK
+N_BLOCKS = EDGES // P
+FLOPS = 2 * EDGES * NODES * CH + 2 * EDGES * CH * CH
+
+V_COLS = (336, 256, 256, 104, 104, 104, 104, 104)
+NF_V = 88
+LOADS = (512, 512, 1024, 1024, 1024)
+W_AFTER = 1
+
+
+def tile_heterogeneoustemporalhypergraphnn_pa_t_kernel(
+    tc, node_features, incidence, W1, b1, edge_attention, out
+):
+    nc = tc.nc
+    with ExitStack() as ctx:
+        const = ctx.enter_context(tc.tile_pool(name="const", bufs=1))
+        ring = ctx.enter_context(tc.tile_pool(name="ring", bufs=3))
+        outs = ctx.enter_context(tc.tile_pool(name="outs", bufs=4))
+        ps1 = ctx.enter_context(tc.psum_pool(name="ps1", bufs=4))
+        ps2 = ctx.enter_context(tc.psum_pool(name="ps2", bufs=4))
+        ctx.enter_context(tc.manual_schedule())
+
+        a_rows = const.tile([N_BLOCKS, P], BF16)
+        nc.scalar.dma_start(out=a_rows[:], in_=edge_attention.rearrange("(k p) -> k p", p=P))
+        b1_one = const.tile([1, CH], BF16)
+        nc.scalar.dma_start(out=b1_one[:], in_=b1.rearrange("(o c) -> o c", o=1))
+        b1row = const.tile([P, CH], BF16)
+        nc.vector.memset(b1row[:], 0.0)
+
+        nf_raw = const.tile([P, PACK, CH], BF16)
+        nc.sync.dma_start(out=nf_raw[:], in_=node_features.rearrange("(q j) c -> q j c", j=PACK))
+        inc_view = incidence.rearrange("(q j) e -> q j e", j=PACK)
+        inc_raw = []
+        w_raw = const.tile([P, PACK, CH], BF16)
+        e0 = 0
+        for li, width in enumerate(LOADS):
+            raw = const.tile([P, PACK, width], BF16, name="inc_raw%d" % li)
+            nc.sync.dma_start(out=raw[:], in_=inc_view[:, :, e0 : e0 + width])
+            for c0 in range(0, width, CHUNK):
+                inc_raw.append((raw, c0))
+            e0 += width
+            if li == W_AFTER:
+                nc.sync.dma_start(out=w_raw[:], in_=W1.rearrange("(q j) c -> q j c", j=PACK))
+
+        ident = const.tile([P, P], F32)
+        make_identity(nc, ident[:])
+        a32 = const.tile([P, P], F32)
+        nc.vector.memset(a32[:], 0.0)
+        ones = const.tile([P, P], BF16)
+        nc.vector.memset(ones[:], 1.0)
+        warm_in = const.tile([P, 1], F32)
+        nc.vector.memset(warm_in[:], 0.0)
+        warm_out = const.tile([P, 1], F32)
+        nc.scalar.activation(out=warm_out[:], in_=warm_in[:], func=ACT.Exp)
+
+        nf_grp = const.tile([P, PACK, P, PACK], BF16, align_bytes=64)
+        nf_codes = const.tile([P, CH], U32, align_bytes=64)
+        nf_scales = const.tile([P, CH], U8, align_bytes=64)
+        w_grp = const.tile([P, CH, PACK], BF16, align_bytes=64)
+        w_codes = const.tile([P, CH], U32, align_bytes=64)
+        w_scales = const.tile([P, CH], U8, align_bytes=64)
+        attn = const.tile([P, N_BLOCKS], F32)
+        b1bc = const.tile([P, CH], F32)
+        b1a = []
+        for g in range(N_CHUNKS):
+            t_b1a = const.tile([P, PACK, CH], F32, name="b1a%d" % g)
+            b1a.append(t_b1a)
+
+        inc_grp = {}
+        inc_codes = {}
+        inc_scales = {}
+        agg_grp = {}
+        agg_codes = {}
+        agg_scales = {}
+        bank2 = {}
+        o_tiles = {}
+
+        def views(grp, raw_ap):
+            dst = grp[:].rearrange("q (c i) j -> q c j i", i=4)
+            src = raw_ap.rearrange("q j (c i) -> q c j i", i=4)
+            return dst, src
+
+        def regroup_s(g):
+            raw, c0 = inc_raw[g]
+            grp = ring.tile([P, CHUNK, PACK], BF16, align_bytes=64, name="inc_grp")
+            inc_grp[g] = grp
+            dst, src = views(grp, raw[:, :, c0 : c0 + CHUNK])
+            cv = V_COLS[g] // 4
+            nc.scalar.copy(out=dst[:, cv:], in_=src[:, cv:])
+
+        def regroup_v(g):
+            raw, c0 = inc_raw[g]
+            dst, src = views(inc_grp[g], raw[:, :, c0 : c0 + CHUNK])
+            cv = V_COLS[g] // 4
+            nc.vector.tensor_copy(out=dst[:, 0:cv], in_=src[:, 0:cv])
+
+        def quant_inc(g):
+            codes = ring.tile([P, CHUNK], U32, align_bytes=64, name="inc_codes")
+            scales = ring.tile([P, CHUNK], U8, align_bytes=64, name="inc_scales")
+            inc_codes[g] = codes
+            inc_scales[g] = scales
+            nc.vector.quantize_mx(
+                out=codes[:].bitcast(FP8X4),
+                scales=scales[:],
+                in_=inc_grp[g][:].rearrange("q e j -> q (e j)"),
+            )
+
+        def stage1(g):
+            grp = ring.tile([P, PACK, P, PACK], BF16, align_bytes=64, name="agg_grp")
+            agg_grp[g] = grp
+            for s in range(4):
+                bank = ps1.tile([P, PACK, P], F32, name="bank1")
+                for t in range(PACK):
+                    nc.tensor.matmul_mx(
+                        out=bank[:, t, :],
+                        lhsT=nf_codes[:, P * t : P * (t + 1)].bitcast(FP8X4),
+                        lhsT_scale=nf_scales[:, P * t : P * (t + 1)],
+                        rhs=inc_codes[g][:, P * s : P * (s + 1)].bitcast(FP8X4),
+                        rhs_scale=inc_scales[g][:, P * s : P * (s + 1)],
+                        start=True,
+                        stop=True,
+                    )
+                nc.scalar.copy(out=grp[:, s, :, :], in_=bank[:].rearrange("c t e -> c e t"))
+
+        def quant_agg(g):
+            codes = ring.tile([P, CHUNK], U32, align_bytes=64, name="agg_codes")
+            scales = ring.tile([P, CHUNK], U8, align_bytes=64, name="agg_scales")
+            agg_codes[g] = codes
+            agg_scales[g] = scales
+            nc.vector.quantize_mx(
+                out=codes[:].bitcast(FP8X4),
+                scales=scales[:],
+                in_=agg_grp[g][:].rearrange("c s e t -> c (s e t)"),
+            )
+
+        out_view = out.rearrange("(k p) c -> p k c", p=P)
+
+        def stage2_mm(g, b):
+            bank = ps2.tile([P, CH], F32, name="bank2")
+            bank2[(g, b)] = bank
+            nc.tensor.matmul_mx(
+                out=bank[:],
+                lhsT=agg_codes[g][:, P * b : P * (b + 1)].bitcast(FP8X4),
+                lhsT_scale=agg_scales[g][:, P * b : P * (b + 1)],
+                rhs=w_codes[:].bitcast(FP8X4),
+                rhs_scale=w_scales[:],
+                start=True,
+                stop=True,
+            )
+
+        def finish(g, b):
+            if b == 0:
+                o_new = outs.tile([P, PACK, CH], F32, name="o")
+                o_tiles[g] = o_new
+            nc.vector.scalar_tensor_tensor(
+                out=o_tiles[g][:, b, :],
+                in0=bank2[(g, b)][:],
+                scalar=attn[:, PACK * g + b : PACK * g + b + 1],
+                in1=b1a[g][:, b, :],
+                op0=ALU.mult,
+                op1=ALU.add,
+            )
+
+        def store(g, b0, nb):
+            nc.sync.dma_start(
+                out=out_view[:, PACK * g + b0 : PACK * g + b0 + nb, :],
+                in_=o_tiles[g][:, b0 : b0 + nb, :],
+            )
+
+        nc.vector.tensor_copy(out=a32[0:N_BLOCKS, :], in_=a_rows[:])
+        tp_a = ps2.tile([P, CH], F32, name="bank2")
+        nc.tensor.transpose(tp_a[:, 0:P], a32[:], ident[:])
+        a_cols = tp_a[:, 0:N_BLOCKS]
+        pmax = const.tile([P, 1], F32)
+        nc.vector.reduce_max(out=pmax[:], in_=a_cols, axis=AX.X)
+        rep_max = const.tile([P, P], F32)
+        nc.vector.tensor_copy(out=rep_max[:], in_=pmax[:].to_broadcast([P, P]))
+        tp_max = ps2.tile([P, CH], F32, name="bank2")
+        nc.tensor.transpose(tp_max[:, 0:P], rep_max[:], ident[:])
+        nc.vector.tensor_copy(out=b1row[0:1, :], in_=b1_one[:])
+        bb = ps2.tile([P, CH], F32, name="bank2")
+        nc.tensor.matmul(out=bb[:], lhsT=ones[:], rhs=b1row[:], start=True, stop=True)
+
+        nf_src = nf_raw[:].rearrange("q j (p t) -> q t p j", t=PACK)
+        nc.vector.tensor_copy(out=nf_grp[:, :, 0:NF_V, :], in_=nf_src[:, :, 0:NF_V, :])
+        nc.scalar.copy(out=nf_grp[:, :, NF_V:P, :], in_=nf_src[:, :, NF_V:P, :])
+
+        gmax = const.tile([P, 1], F32)
+        nc.vector.reduce_max(out=gmax[:], in_=tp_max[:, 0:P], axis=AX.X)
+        ngmax = const.tile([P, 1], F32)
+        nc.vector.tensor_scalar_mul(ngmax[:], gmax[:], -1.0)
+        ex = const.tile([P, N_BLOCKS], F32)
+        psumx = const.tile([P, 1], F32)
+        nc.scalar.activation(
+            out=ex[:], in_=a_cols, func=ACT.Exp, bias=ngmax[:], scale=1.0, accum_out=psumx[:]
+        )
+
+        nc.vector.quantize_mx(
+            out=nf_codes[:].bitcast(FP8X4),
+            scales=nf_scales[:],
+            in_=nf_grp[:].rearrange("q t p j -> q (t p j)"),
+        )
+        regroup_s(0)
+        nc.scalar.copy(out=b1bc[:], in_=bb[:])
+        rep_sum = const.tile([P, P], F32)
+        nc.vector.tensor_copy(out=rep_sum[:], in_=psumx[:].to_broadcast([P, P]))
+        tp_sum = ps2.tile([P, CH], F32, name="bank2")
+        nc.tensor.transpose(tp_sum[:, 0:P], rep_sum[:], ident[:])
+        regroup_v(0)
+        gsum = const.tile([P, 1], F32)
+        nc.vector.reduce_sum(out=gsum[:], in_=tp_sum[:, 0:P], axis=AX.X)
+        rsum = const.tile([P, 1], F32)
+        nc.vector.reciprocal(out=rsum[:], in_=gsum[:])
+        nc.vector.tensor_scalar_mul(attn[:], ex[:], rsum[:])
+        for k in range(N_BLOCKS):
+            nc.gpsimd.tensor_scalar(
+                out=b1a[k // PACK][:, k % PACK, :],
+                in0=b1bc[:],
+                scalar1=attn[:, k : k + 1],
+                scalar2=0.0,
+                op0=ALU.mult,
+                op1=ALU.add,
+            )
+        quant_inc(0)
+
+        w_dst, w_src = views(w_grp, w_raw[:])
+        for i in range(-1, N_CHUNKS + 1):
+            if i + 2 < N_CHUNKS:
+                regroup_s(i + 2)
+            if i + 1 < N_CHUNKS:
+                stage1(i + 1)
+            if 0 <= i < N_CHUNKS:
+                quant_agg(i)
+                stage2_mm(i, 0)
+                stage2_mm(i, 1)
+            if i >= 1:
+                finish(i - 1, 2)
+                finish(i - 1, 3)
+                if i - 1 == N_CHUNKS - 1:
+                    store(i - 1, 2, 2)
+                else:
+                    store(i - 1, 0, 4)
+            if 0 <= i < N_CHUNKS:
+                stage2_mm(i, 2)
+                stage2_mm(i, 3)
+            if i + 2 < N_CHUNKS:
+                regroup_v(i + 2)
+            if i == -1:
+                nc.vector.tensor_copy(out=w_dst, in_=w_src)
+                quant_inc(1)
+            if 0 <= i < N_CHUNKS:
+                finish(i, 0)
+                finish(i, 1)
+                if i == N_CHUNKS - 1:
+                    store(i, 0, 2)
+            if 0 <= i and i + 2 < N_CHUNKS:
+                quant_inc(i + 2)
+            if i == -1:
+                nc.vector.quantize_mx(
+                    out=w_codes[:].bitcast(FP8X4),
+                    scales=w_scales[:],
+                    in_=w_grp[:].rearrange("q c j -> q (c j)"),
+                )

@@ -26,6 +26,7 @@ V_COLS = (336, 256, 256, 104, 104, 104, 104, 104)
 NF_V = 88
 LOADS = (512, 512, 1024, 1024, 1024)
 W_AFTER = 1
+STORE_BLOCKS = (4, 4, 4, 4, 4, 2, 2, 1)
 
 
 def tile_heterogeneoustemporalhypergraphnn_pa_t_kernel(
@@ -180,12 +181,13 @@ def tile_heterogeneoustemporalhypergraphnn_pa_t_kernel(
                 op0=ALU.mult,
                 op1=ALU.add,
             )
-
-        def store(g, b0, nb):
-            nc.sync.dma_start(
-                out=out_view[:, PACK * g + b0 : PACK * g + b0 + nb, :],
-                in_=o_tiles[g][:, b0 : b0 + nb, :],
-            )
+            nb = STORE_BLOCKS[g]
+            if (b + 1) % nb == 0:
+                b0 = b + 1 - nb
+                nc.sync.dma_start(
+                    out=out_view[:, PACK * g + b0 : PACK * g + b0 + nb, :],
+                    in_=o_tiles[g][:, b0 : b0 + nb, :],
+                )
 
         nc.vector.tensor_copy(out=a32[0:N_BLOCKS, :], in_=a_rows[:])
         tp_a = ps2.tile([P, CH], F32, name="bank2")
@@ -256,10 +258,6 @@ def tile_heterogeneoustemporalhypergraphnn_pa_t_kernel(
             if i >= 1:
                 finish(i - 1, 2)
                 finish(i - 1, 3)
-                if i - 1 == N_CHUNKS - 1:
-                    store(i - 1, 2, 2)
-                else:
-                    store(i - 1, 0, 4)
             if 0 <= i < N_CHUNKS:
                 stage2_mm(i, 2)
                 stage2_mm(i, 3)
@@ -271,8 +269,6 @@ def tile_heterogeneoustemporalhypergraphnn_pa_t_kernel(
             if 0 <= i < N_CHUNKS:
                 finish(i, 0)
                 finish(i, 1)
-                if i == N_CHUNKS - 1:
-                    store(i, 0, 2)
             if 0 <= i and i + 2 < N_CHUNKS:
                 quant_inc(i + 2)
             if i == -1:

@@ -22,7 +22,8 @@ N_CHUNKS = EDGES // CHUNK
 N_BLOCKS = EDGES // P
 FLOPS = 2 * EDGES * NODES * CH + 2 * EDGES * CH * CH
 
-V_COLS = (336, 256, 256, 104, 104, 104, 104, 104)
+V_COLS = (336, 256, 256, 0, 0, 0, 0, 0)
+V_EXITS = (0, 1, 0, 1, 0, 1, 0, 0)
 NF_V = 88
 LOADS = (512, 512, 1024, 1024, 1024)
 W_AFTER = 1
@@ -93,6 +94,7 @@ def tile_heterogeneoustemporalhypergraphnn_pa_t_kernel(
         agg_grp = {}
         agg_codes = {}
         agg_scales = {}
+        bank1 = {}
         bank2 = {}
         o_tiles = {}
 
@@ -113,7 +115,8 @@ def tile_heterogeneoustemporalhypergraphnn_pa_t_kernel(
             raw, c0 = inc_raw[g]
             dst, src = views(inc_grp[g], raw[:, :, c0 : c0 + CHUNK])
             cv = V_COLS[g] // 4
-            nc.vector.tensor_copy(out=dst[:, 0:cv], in_=src[:, 0:cv])
+            if cv > 0:
+                nc.vector.tensor_copy(out=dst[:, 0:cv], in_=src[:, 0:cv])
 
         def quant_inc(g):
             codes = ring.tile([P, CHUNK], U32, align_bytes=64, name="inc_codes")
@@ -141,7 +144,16 @@ def tile_heterogeneoustemporalhypergraphnn_pa_t_kernel(
                         start=True,
                         stop=True,
                     )
-                nc.scalar.copy(out=grp[:, s, :, :], in_=bank[:].rearrange("c t e -> c e t"))
+                bank1[(g, s)] = bank
+                if s < 4 - V_EXITS[g]:
+                    nc.scalar.copy(out=grp[:, s, :, :], in_=bank[:].rearrange("c t e -> c e t"))
+
+        def stage1_exits_v(g):
+            for s in range(4 - V_EXITS[g], 4):
+                nc.vector.tensor_copy(
+                    out=agg_grp[g][:, s, :, :],
+                    in_=bank1[(g, s)][:].rearrange("c t e -> c e t"),
+                )
 
         def quant_agg(g):
             codes = ring.tile([P, CHUNK], U32, align_bytes=64, name="agg_codes")
@@ -266,6 +278,8 @@ def tile_heterogeneoustemporalhypergraphnn_pa_t_kernel(
             if i == -1:
                 nc.vector.tensor_copy(out=w_dst, in_=w_src)
                 quant_inc(1)
+            if i + 1 < N_CHUNKS:
+                stage1_exits_v(i + 1)
             if 0 <= i < N_CHUNKS:
                 finish(i, 0)
                 finish(i, 1)

@@ -129,9 +129,7 @@ def tile_heterogeneoustemporalhypergraphnn_pa_t_kernel(
                 in_=inc_grp[g][:].rearrange("q e j -> q (e j)"),
             )
 
-        def stage1(g):
-            grp = ring.tile([P, PACK, P, PACK], BF16, align_bytes=64, name="agg_grp")
-            agg_grp[g] = grp
+        def stage1_mm(g):
             for s in range(4):
                 bank = ps1.tile([P, PACK, P], F32, name="bank1")
                 for t in range(PACK):
@@ -145,8 +143,14 @@ def tile_heterogeneoustemporalhypergraphnn_pa_t_kernel(
                         stop=True,
                     )
                 bank1[(g, s)] = bank
-                if s < 4 - V_EXITS[g]:
-                    nc.scalar.copy(out=grp[:, s, :, :], in_=bank[:].rearrange("c t e -> c e t"))
+
+        def stage1_exits_s(g):
+            grp = ring.tile([P, PACK, P, PACK], BF16, align_bytes=64, name="agg_grp")
+            agg_grp[g] = grp
+            for s in range(4 - V_EXITS[g]):
+                nc.scalar.copy(
+                    out=grp[:, s, :, :], in_=bank1[(g, s)][:].rearrange("c t e -> c e t")
+                )
 
         def stage1_exits_v(g):
             for s in range(4 - V_EXITS[g], 4):
@@ -258,36 +262,40 @@ def tile_heterogeneoustemporalhypergraphnn_pa_t_kernel(
         quant_inc(0)
 
         w_dst, w_src = views(w_grp, w_raw[:])
-        for i in range(-1, N_CHUNKS + 1):
-            if i + 2 < N_CHUNKS:
-                regroup_s(i + 2)
-            if i + 1 < N_CHUNKS:
-                stage1(i + 1)
-            if 0 <= i < N_CHUNKS:
+        stage1_mm(0)
+        regroup_s(1)
+        regroup_v(1)
+        nc.vector.tensor_copy(out=w_dst, in_=w_src)
+        quant_inc(1)
+        nc.vector.quantize_mx(
+            out=w_codes[:].bitcast(FP8X4),
+            scales=w_scales[:],
+            in_=w_grp[:].rearrange("q c j -> q (c j)"),
+        )
+        stage1_exits_s(0)
+        stage1_exits_v(0)
+        stage1_mm(1)
+        regroup_s(2)
+        regroup_v(2)
+        for i in range(N_CHUNKS + 1):
+            if i < N_CHUNKS:
                 quant_agg(i)
                 stage2_mm(i, 0)
-                stage2_mm(i, 1)
-            if i >= 1:
-                finish(i - 1, 2)
-                finish(i - 1, 3)
-            if 0 <= i < N_CHUNKS:
-                stage2_mm(i, 2)
-                stage2_mm(i, 3)
+            if i + 1 < N_CHUNKS:
+                stage1_exits_s(i + 1)
+            for b in range(1, PACK):
+                if i >= 1:
+                    finish(i - 1, b)
+                if i < N_CHUNKS:
+                    stage2_mm(i, b)
+            if i + 3 < N_CHUNKS:
+                regroup_s(i + 3)
+                regroup_v(i + 3)
             if i + 2 < N_CHUNKS:
-                regroup_v(i + 2)
-            if i == -1:
-                nc.vector.tensor_copy(out=w_dst, in_=w_src)
-                quant_inc(1)
+                quant_inc(i + 2)
             if i + 1 < N_CHUNKS:
                 stage1_exits_v(i + 1)
-            if 0 <= i < N_CHUNKS:
+            if i + 2 < N_CHUNKS:
+                stage1_mm(i + 2)
+            if i < N_CHUNKS:
                 finish(i, 0)
-                finish(i, 1)
-            if 0 <= i and i + 2 < N_CHUNKS:
-                quant_inc(i + 2)
-            if i == -1:
-                nc.vector.quantize_mx(
-                    out=w_codes[:].bitcast(FP8X4),
-                    scales=w_scales[:],
-                    in_=w_grp[:].rearrange("q c j -> q (c j)"),
-                )

@@ -22,9 +22,8 @@ N_CHUNKS = EDGES // CHUNK
 N_BLOCKS = EDGES // P
 FLOPS = 2 * EDGES * NODES * CH + 2 * EDGES * CH * CH
 
-V_COLS = (336, 256, 256, 0, 0, 0, 0, 0)
-V_EXITS = (0, 1, 0, 1, 0, 1, 0, 0)
-NF_V = 88
+V_COLS = (320, 384, 192, 192, 192, 192, 192, 128)
+V_EXITS = (1, 0, 0, 0, 0, 0, 0, 0)
 LOADS = (512, 512, 1024, 1024, 1024)
 W_AFTER = 1
 STORE_BLOCKS = (4, 4, 4, 4, 4, 2, 2, 1)
@@ -49,8 +48,12 @@ def tile_heterogeneoustemporalhypergraphnn_pa_t_kernel(
         b1row = const.tile([P, CH], BF16)
         nc.vector.memset(b1row[:], 0.0)
 
-        nf_raw = const.tile([P, PACK, CH], BF16)
-        nc.sync.dma_start(out=nf_raw[:], in_=node_features.rearrange("(q j) c -> q j c", j=PACK))
+        nf_view = node_features.rearrange("(q j) c -> q j c", j=PACK)
+        nf_raw = []
+        for h in range(2):
+            raw = const.tile([P, PACK, CH // 2], BF16, name="nf_raw%d" % h)
+            nc.sync.dma_start(out=raw[:], in_=nf_view[:, :, CH // 2 * h : CH // 2 * (h + 1)])
+            nf_raw.append(raw)
         inc_view = incidence.rearrange("(q j) e -> q j e", j=PACK)
         inc_raw = []
         w_raw = const.tile([P, PACK, CH], BF16)
@@ -205,51 +208,49 @@ def tile_heterogeneoustemporalhypergraphnn_pa_t_kernel(
                     in_=o_tiles[g][:, b0 : b0 + nb, :],
                 )
 
-        nc.vector.tensor_copy(out=a32[0:N_BLOCKS, :], in_=a_rows[:])
+        def nf_views(h):
+            src = nf_raw[h][:].rearrange("q j (p t) -> q t p j", t=PACK)
+            o = P // 2 * h
+            return nf_grp[:, :, o : o + P // 2, :], src
+
+        nc.vector.tensor_scalar_mul(a32[0:N_BLOCKS, :], a_rows[:], -1.0)
         tp_a = ps2.tile([P, CH], F32, name="bank2")
         nc.tensor.transpose(tp_a[:, 0:P], a32[:], ident[:])
         a_cols = tp_a[:, 0:N_BLOCKS]
-        pmax = const.tile([P, 1], F32)
-        nc.vector.reduce_max(out=pmax[:], in_=a_cols, axis=AX.X)
-        rep_max = const.tile([P, P], F32)
-        nc.vector.tensor_copy(out=rep_max[:], in_=pmax[:].to_broadcast([P, P]))
-        tp_max = ps2.tile([P, CH], F32, name="bank2")
-        nc.tensor.transpose(tp_max[:, 0:P], rep_max[:], ident[:])
+        pmin = const.tile([P, 1], F32)
+        nc.vector.tensor_reduce(out=pmin[:], in_=a_cols, axis=AX.X, op=ALU.min)
+        tp_min = ps2.tile([P, CH], F32, name="bank2")
+        nc.tensor.transpose(tp_min[:, 0:P], pmin[:].to_broadcast([P, P]), ident[:])
         nc.vector.tensor_copy(out=b1row[0:1, :], in_=b1_one[:])
         bb = ps2.tile([P, CH], F32, name="bank2")
         nc.tensor.matmul(out=bb[:], lhsT=ones[:], rhs=b1row[:], start=True, stop=True)
 
-        nf_src = nf_raw[:].rearrange("q j (p t) -> q t p j", t=PACK)
-        nc.vector.tensor_copy(out=nf_grp[:, :, 0:NF_V, :], in_=nf_src[:, :, 0:NF_V, :])
-        nc.scalar.copy(out=nf_grp[:, :, NF_V:P, :], in_=nf_src[:, :, NF_V:P, :])
-
-        gmax = const.tile([P, 1], F32)
-        nc.vector.reduce_max(out=gmax[:], in_=tp_max[:, 0:P], axis=AX.X)
+        dst, src = nf_views(0)
+        nc.vector.tensor_copy(out=dst, in_=src)
         ngmax = const.tile([P, 1], F32)
-        nc.vector.tensor_scalar_mul(ngmax[:], gmax[:], -1.0)
+        nc.vector.tensor_reduce(out=ngmax[:], in_=tp_min[:, 0:P], axis=AX.X, op=ALU.min)
         ex = const.tile([P, N_BLOCKS], F32)
         psumx = const.tile([P, 1], F32)
         nc.scalar.activation(
-            out=ex[:], in_=a_cols, func=ACT.Exp, bias=ngmax[:], scale=1.0, accum_out=psumx[:]
+            out=ex[:], in_=a_cols, func=ACT.Exp, bias=ngmax[:], scale=-1.0, accum_out=psumx[:]
         )
-
+        tp_sum = ps2.tile([P, CH], F32, name="bank2")
+        nc.tensor.transpose(tp_sum[:, 0:P], psumx[:].to_broadcast([P, P]), ident[:])
+        dst, src = nf_views(1)
+        nc.vector.tensor_copy(out=dst, in_=src)
+        nc.scalar.copy(out=b1bc[:], in_=bb[:])
+        gsum = const.tile([P, 1], F32)
+        nc.vector.reduce_sum(out=gsum[:], in_=tp_sum[:, 0:P], axis=AX.X)
+        rsum = const.tile([P, 1], F32)
+        nc.vector.reciprocal(out=rsum[:], in_=gsum[:])
         nc.vector.quantize_mx(
             out=nf_codes[:].bitcast(FP8X4),
             scales=nf_scales[:],
             in_=nf_grp[:].rearrange("q t p j -> q (t p j)"),
         )
-        regroup_s(0)
-        nc.scalar.copy(out=b1bc[:], in_=bb[:])
-        rep_sum = const.tile([P, P], F32)
-        nc.vector.tensor_copy(out=rep_sum[:], in_=psumx[:].to_broadcast([P, P]))
-        tp_sum = ps2.tile([P, CH], F32, name="bank2")
-        nc.tensor.transpose(tp_sum[:, 0:P], rep_sum[:], ident[:])
-        regroup_v(0)
-        gsum = const.tile([P, 1], F32)
-        nc.vector.reduce_sum(out=gsum[:], in_=tp_sum[:, 0:P], axis=AX.X)
-        rsum = const.tile([P, 1], F32)
-        nc.vector.reciprocal(out=rsum[:], in_=gsum[:])
         nc.vector.tensor_scalar_mul(attn[:], ex[:], rsum[:])
+        regroup_s(0)
+        regroup_v(0)
         for k in range(N_BLOCKS):
             nc.gpsimd.tensor_scalar(
                 out=b1a[k // PACK][:, k % PACK, :],
@@ -265,7 +266,7 @@ def tile_heterogeneoustemporalhypergraphnn_pa_t_kernel(
         stage1_mm(0)
         regroup_s(1)
         regroup_v(1)
-        nc.vector.tensor_copy(out=w_dst, in_=w_src)
+        nc.scalar.copy(out=w_dst, in_=w_src)
         quant_inc(1)
         nc.vector.quantize_mx(
             out=w_codes[:].bitcast(FP8X4),

@@ -22,7 +22,7 @@ N_CHUNKS = EDGES // CHUNK
 N_BLOCKS = EDGES // P
 FLOPS = 2 * EDGES * NODES * CH + 2 * EDGES * CH * CH
 
-V_COLS = (320, 384, 192, 192, 192, 192, 192, 128)
+V_COLS = (256, 384, 160, 160, 160, 160, 160, 0)
 V_EXITS = (1, 0, 0, 0, 0, 0, 0, 0)
 LOADS = (512, 512, 1024, 1024, 1024)
 W_AFTER = 1
@@ -36,7 +36,7 @@ def tile_heterogeneoustemporalhypergraphnn_pa_t_kernel(
     with ExitStack() as ctx:
         const = ctx.enter_context(tc.tile_pool(name="const", bufs=1))
         ring = ctx.enter_context(tc.tile_pool(name="ring", bufs=3))
-        outs = ctx.enter_context(tc.tile_pool(name="outs", bufs=4))
+        quant = ctx.enter_context(tc.tile_pool(name="quant", bufs=N_CHUNKS))
         ps1 = ctx.enter_context(tc.psum_pool(name="ps1", bufs=4))
         ps2 = ctx.enter_context(tc.psum_pool(name="ps2", bufs=4))
         ctx.enter_context(tc.manual_schedule())
@@ -99,7 +99,6 @@ def tile_heterogeneoustemporalhypergraphnn_pa_t_kernel(
         agg_scales = {}
         bank1 = {}
         bank2 = {}
-        o_tiles = {}
 
         def views(grp, raw_ap):
             dst = grp[:].rearrange("q (c i) j -> q c j i", i=4)
@@ -122,8 +121,8 @@ def tile_heterogeneoustemporalhypergraphnn_pa_t_kernel(
                 nc.vector.tensor_copy(out=dst[:, 0:cv], in_=src[:, 0:cv])
 
         def quant_inc(g):
-            codes = ring.tile([P, CHUNK], U32, align_bytes=64, name="inc_codes")
-            scales = ring.tile([P, CHUNK], U8, align_bytes=64, name="inc_scales")
+            codes = quant.tile([P, CHUNK], U32, align_bytes=64, name="inc_codes")
+            scales = quant.tile([P, CHUNK], U8, align_bytes=64, name="inc_scales")
             inc_codes[g] = codes
             inc_scales[g] = scales
             nc.vector.quantize_mx(
@@ -163,8 +162,8 @@ def tile_heterogeneoustemporalhypergraphnn_pa_t_kernel(
                 )
 
         def quant_agg(g):
-            codes = ring.tile([P, CHUNK], U32, align_bytes=64, name="agg_codes")
-            scales = ring.tile([P, CHUNK], U8, align_bytes=64, name="agg_scales")
+            codes = quant.tile([P, CHUNK], U32, align_bytes=64, name="agg_codes")
+            scales = quant.tile([P, CHUNK], U8, align_bytes=64, name="agg_scales")
             agg_codes[g] = codes
             agg_scales[g] = scales
             nc.vector.quantize_mx(
@@ -189,11 +188,8 @@ def tile_heterogeneoustemporalhypergraphnn_pa_t_kernel(
             )
 
         def finish(g, b):
-            if b == 0:
-                o_new = outs.tile([P, PACK, CH], F32, name="o")
-                o_tiles[g] = o_new
             nc.vector.scalar_tensor_tensor(
-                out=o_tiles[g][:, b, :],
+                out=b1a[g][:, b, :],
                 in0=bank2[(g, b)][:],
                 scalar=attn[:, PACK * g + b : PACK * g + b + 1],
                 in1=b1a[g][:, b, :],
@@ -205,7 +201,7 @@ def tile_heterogeneoustemporalhypergraphnn_pa_t_kernel(
                 b0 = b + 1 - nb
                 nc.sync.dma_start(
                     out=out_view[:, PACK * g + b0 : PACK * g + b0 + nb, :],
-                    in_=o_tiles[g][:, b0 : b0 + nb, :],
+                    in_=b1a[g][:, b0 : b0 + nb, :],
                 )
 
         def nf_views(h):
@@ -251,7 +247,7 @@ def tile_heterogeneoustemporalhypergraphnn_pa_t_kernel(
         nc.vector.tensor_scalar_mul(attn[:], ex[:], rsum[:])
         regroup_s(0)
         regroup_v(0)
-        for k in range(N_BLOCKS):
+        for k in range(N_BLOCKS - PACK):
             nc.gpsimd.tensor_scalar(
                 out=b1a[k // PACK][:, k % PACK, :],
                 in0=b1bc[:],
@@ -279,12 +275,23 @@ def tile_heterogeneoustemporalhypergraphnn_pa_t_kernel(
         regroup_s(2)
         regroup_v(2)
         for i in range(N_CHUNKS + 1):
+            if i >= 1:
+                finish(i - 1, 1)
             if i < N_CHUNKS:
                 quant_agg(i)
                 stage2_mm(i, 0)
+                stage2_mm(i, 1)
             if i + 1 < N_CHUNKS:
                 stage1_exits_s(i + 1)
-            for b in range(1, PACK):
+            if i + 2 == N_CHUNKS:
+                for b in range(PACK):
+                    nc.scalar.activation(
+                        out=b1a[i + 1][:, b, :],
+                        in_=b1bc[:],
+                        func=ACT.Copy,
+                        scale=attn[:, PACK * (i + 1) + b : PACK * (i + 1) + b + 1],
+                    )
+            for b in range(2, PACK):
                 if i >= 1:
                     finish(i - 1, b)
                 if i < N_CHUNKS:

from contextlib import ExitStack

import concourse.mybir as mybir
from concourse.masks import make_identity

F32 = mybir.dt.float32
BF16 = mybir.dt.bfloat16
U32 = mybir.dt.uint32
U8 = mybir.dt.uint8
FP8X4 = mybir.dt.float8_e4m3fn_x4
ALU = mybir.AluOpType
ACT = mybir.ActivationFunctionType
AX = mybir.AxisListType

P = 128
PACK = 4
NODES = 512
EDGES = 4096
CH = 512
CHUNK = 512
N_CHUNKS = EDGES // CHUNK
N_BLOCKS = EDGES // P
FLOPS = 2 * EDGES * NODES * CH + 2 * EDGES * CH * CH

V_COLS = (256, 384, 160, 160, 160, 160, 160, 0)
V_EXITS = (1, 0, 0, 0, 0, 0, 0, 0)
LOADS = (512, 512, 1024, 1024, 1024)
W_AFTER = 1
STORE_BLOCKS = (4, 4, 4, 4, 4, 2, 2, 1)


def tile_heterogeneoustemporalhypergraphnn_pa_t_kernel(
    tc, node_features, incidence, W1, b1, edge_attention, out
):
    nc = tc.nc
    with ExitStack() as ctx:
        const = ctx.enter_context(tc.tile_pool(name="const", bufs=1))
        ring = ctx.enter_context(tc.tile_pool(name="ring", bufs=3))
        quant = ctx.enter_context(tc.tile_pool(name="quant", bufs=N_CHUNKS))
        ps1 = ctx.enter_context(tc.psum_pool(name="ps1", bufs=4))
        ps2 = ctx.enter_context(tc.psum_pool(name="ps2", bufs=4))
        ctx.enter_context(tc.manual_schedule())

        a_rows = const.tile([N_BLOCKS, P], BF16)
        nc.scalar.dma_start(out=a_rows[:], in_=edge_attention.rearrange("(k p) -> k p", p=P))
        b1_one = const.tile([1, CH], BF16)
        nc.scalar.dma_start(out=b1_one[:], in_=b1.rearrange("(o c) -> o c", o=1))
        b1row = const.tile([P, CH], BF16)
        nc.vector.memset(b1row[:], 0.0)

        nf_view = node_features.rearrange("(q j) c -> q j c", j=PACK)
        nf_raw = []
        for h in range(2):
            raw = const.tile([P, PACK, CH // 2], BF16, name="nf_raw%d" % h)
            nc.sync.dma_start(out=raw[:], in_=nf_view[:, :, CH // 2 * h : CH // 2 * (h + 1)])
            nf_raw.append(raw)
        inc_view = incidence.rearrange("(q j) e -> q j e", j=PACK)
        inc_raw = []
        w_raw = const.tile([P, PACK, CH], BF16)
        e0 = 0
        for li, width in enumerate(LOADS):
            raw = const.tile([P, PACK, width], BF16, name="inc_raw%d" % li)
            nc.sync.dma_start(out=raw[:], in_=inc_view[:, :, e0 : e0 + width])
            for c0 in range(0, width, CHUNK):
                inc_raw.append((raw, c0))
            e0 += width
            if li == W_AFTER:
                nc.sync.dma_start(out=w_raw[:], in_=W1.rearrange("(q j) c -> q j c", j=PACK))

        ident = const.tile([P, P], F32)
        make_identity(nc, ident[:])
        a32 = const.tile([P, P], F32)
        nc.vector.memset(a32[:], 0.0)
        ones = const.tile([P, P], BF16)
        nc.vector.memset(ones[:], 1.0)
        warm_in = const.tile([P, 1], F32)
        nc.vector.memset(warm_in[:], 0.0)
        warm_out = const.tile([P, 1], F32)
        nc.scalar.activation(out=warm_out[:], in_=warm_in[:], func=ACT.Exp)

        nf_grp = const.tile([P, PACK, P, PACK], BF16, align_bytes=64)
        nf_codes = const.tile([P, CH], U32, align_bytes=64)
        nf_scales = const.tile([P, CH], U8, align_bytes=64)
        w_grp = const.tile([P, CH, PACK], BF16, align_bytes=64)
        w_codes = const.tile([P, CH], U32, align_bytes=64)
        w_scales = const.tile([P, CH], U8, align_bytes=64)
        attn = const.tile([P, N_BLOCKS], F32)
        b1bc = const.tile([P, CH], F32)
        b1a = []
        for g in range(N_CHUNKS):
            t_b1a = const.tile([P, PACK, CH], F32, name="b1a%d" % g)
            b1a.append(t_b1a)

        inc_grp = {}
        inc_codes = {}
        inc_scales = {}
        agg_grp = {}
        agg_codes = {}
        agg_scales = {}
        bank1 = {}
        bank2 = {}

        def views(grp, raw_ap):
            dst = grp[:].rearrange("q (c i) j -> q c j i", i=4)
            src = raw_ap.rearrange("q j (c i) -> q c j i", i=4)
            return dst, src

        def regroup_s(g):
            raw, c0 = inc_raw[g]
            grp = ring.tile([P, CHUNK, PACK], BF16, align_bytes=64, name="inc_grp")
            inc_grp[g] = grp
            dst, src = views(grp, raw[:, :, c0 : c0 + CHUNK])
            cv = V_COLS[g] // 4
            nc.scalar.copy(out=dst[:, cv:], in_=src[:, cv:])

        def regroup_v(g):
            raw, c0 = inc_raw[g]
            dst, src = views(inc_grp[g], raw[:, :, c0 : c0 + CHUNK])
            cv = V_COLS[g] // 4
            if cv > 0:
                nc.vector.tensor_copy(out=dst[:, 0:cv], in_=src[:, 0:cv])

        def quant_inc(g):
            codes = quant.tile([P, CHUNK], U32, align_bytes=64, name="inc_codes")
            scales = quant.tile([P, CHUNK], U8, align_bytes=64, name="inc_scales")
            inc_codes[g] = codes
            inc_scales[g] = scales
            nc.vector.quantize_mx(
                out=codes[:].bitcast(FP8X4),
                scales=scales[:],
                in_=inc_grp[g][:].rearrange("q e j -> q (e j)"),
            )

        def stage1_mm(g):
            for s in range(4):
                bank = ps1.tile([P, PACK, P], F32, name="bank1")
                for t in range(PACK):
                    nc.tensor.matmul_mx(
                        out=bank[:, t, :],
                        lhsT=nf_codes[:, P * t : P * (t + 1)].bitcast(FP8X4),
                        lhsT_scale=nf_scales[:, P * t : P * (t + 1)],
                        rhs=inc_codes[g][:, P * s : P * (s + 1)].bitcast(FP8X4),
                        rhs_scale=inc_scales[g][:, P * s : P * (s + 1)],
                        start=True,
                        stop=True,
                    )
                bank1[(g, s)] = bank

        def stage1_exits_s(g):
            grp = ring.tile([P, PACK, P, PACK], BF16, align_bytes=64, name="agg_grp")
            agg_grp[g] = grp
            for s in range(4 - V_EXITS[g]):
                nc.scalar.copy(
                    out=grp[:, s, :, :], in_=bank1[(g, s)][:].rearrange("c t e -> c e t")
                )

        def stage1_exits_v(g):
            for s in range(4 - V_EXITS[g], 4):
                nc.vector.tensor_copy(
                    out=agg_grp[g][:, s, :, :],
                    in_=bank1[(g, s)][:].rearrange("c t e -> c e t"),
                )

        def quant_agg(g):
            codes = quant.tile([P, CHUNK], U32, align_bytes=64, name="agg_codes")
            scales = quant.tile([P, CHUNK], U8, align_bytes=64, name="agg_scales")
            agg_codes[g] = codes
            agg_scales[g] = scales
            nc.vector.quantize_mx(
                out=codes[:].bitcast(FP8X4),
                scales=scales[:],
                in_=agg_grp[g][:].rearrange("c s e t -> c (s e t)"),
            )

        out_view = out.rearrange("(k p) c -> p k c", p=P)

        def stage2_mm(g, b):
            bank = ps2.tile([P, CH], F32, name="bank2")
            bank2[(g, b)] = bank
            nc.tensor.matmul_mx(
                out=bank[:],
                lhsT=agg_codes[g][:, P * b : P * (b + 1)].bitcast(FP8X4),
                lhsT_scale=agg_scales[g][:, P * b : P * (b + 1)],
                rhs=w_codes[:].bitcast(FP8X4),
                rhs_scale=w_scales[:],
                start=True,
                stop=True,
            )

        def finish(g, b):
            nc.vector.scalar_tensor_tensor(
                out=b1a[g][:, b, :],
                in0=bank2[(g, b)][:],
                scalar=attn[:, PACK * g + b : PACK * g + b + 1],
                in1=b1a[g][:, b, :],
                op0=ALU.mult,
                op1=ALU.add,
            )
            nb = STORE_BLOCKS[g]
            if (b + 1) % nb == 0:
                b0 = b + 1 - nb
                nc.sync.dma_start(
                    out=out_view[:, PACK * g + b0 : PACK * g + b0 + nb, :],
                    in_=b1a[g][:, b0 : b0 + nb, :],
                )

        def nf_views(h):
            src = nf_raw[h][:].rearrange("q j (p t) -> q t p j", t=PACK)
            o = P // 2 * h
            return nf_grp[:, :, o : o + P // 2, :], src

        nc.vector.tensor_scalar_mul(a32[0:N_BLOCKS, :], a_rows[:], -1.0)
        tp_a = ps2.tile([P, CH], F32, name="bank2")
        nc.tensor.transpose(tp_a[:, 0:P], a32[:], ident[:])
        a_cols = tp_a[:, 0:N_BLOCKS]
        pmin = const.tile([P, 1], F32)
        nc.vector.tensor_reduce(out=pmin[:], in_=a_cols, axis=AX.X, op=ALU.min)
        tp_min = ps2.tile([P, CH], F32, name="bank2")
        nc.tensor.transpose(tp_min[:, 0:P], pmin[:].to_broadcast([P, P]), ident[:])
        nc.vector.tensor_copy(out=b1row[0:1, :], in_=b1_one[:])
        bb = ps2.tile([P, CH], F32, name="bank2")
        nc.tensor.matmul(out=bb[:], lhsT=ones[:], rhs=b1row[:], start=True, stop=True)

        dst, src = nf_views(0)
        nc.vector.tensor_copy(out=dst, in_=src)
        ngmax = const.tile([P, 1], F32)
        nc.vector.tensor_reduce(out=ngmax[:], in_=tp_min[:, 0:P], axis=AX.X, op=ALU.min)
        ex = const.tile([P, N_BLOCKS], F32)
        psumx = const.tile([P, 1], F32)
        nc.scalar.activation(
            out=ex[:], in_=a_cols, func=ACT.Exp, bias=ngmax[:], scale=-1.0, accum_out=psumx[:]
        )
        tp_sum = ps2.tile([P, CH], F32, name="bank2")
        nc.tensor.transpose(tp_sum[:, 0:P], psumx[:].to_broadcast([P, P]), ident[:])
        dst, src = nf_views(1)
        nc.vector.tensor_copy(out=dst, in_=src)
        nc.scalar.copy(out=b1bc[:], in_=bb[:])
        gsum = const.tile([P, 1], F32)
        nc.vector.reduce_sum(out=gsum[:], in_=tp_sum[:, 0:P], axis=AX.X)
        rsum = const.tile([P, 1], F32)
        nc.vector.reciprocal(out=rsum[:], in_=gsum[:])
        nc.vector.quantize_mx(
            out=nf_codes[:].bitcast(FP8X4),
            scales=nf_scales[:],
            in_=nf_grp[:].rearrange("q t p j -> q (t p j)"),
        )
        nc.vector.tensor_scalar_mul(attn[:], ex[:], rsum[:])
        regroup_s(0)
        regroup_v(0)
        for k in range(N_BLOCKS - PACK):
            nc.gpsimd.tensor_scalar(
                out=b1a[k // PACK][:, k % PACK, :],
                in0=b1bc[:],
                scalar1=attn[:, k : k + 1],
                scalar2=0.0,
                op0=ALU.mult,
                op1=ALU.add,
            )
        quant_inc(0)

        w_dst, w_src = views(w_grp, w_raw[:])
        stage1_mm(0)
        regroup_s(1)
        regroup_v(1)
        nc.scalar.copy(out=w_dst, in_=w_src)
        quant_inc(1)
        nc.vector.quantize_mx(
            out=w_codes[:].bitcast(FP8X4),
            scales=w_scales[:],
            in_=w_grp[:].rearrange("q c j -> q (c j)"),
        )
        stage1_exits_s(0)
        stage1_exits_v(0)
        stage1_mm(1)
        regroup_s(2)
        regroup_v(2)
        for i in range(N_CHUNKS + 1):
            if i >= 1:
                finish(i - 1, 1)
            if i < N_CHUNKS:
                quant_agg(i)
                stage2_mm(i, 0)
                stage2_mm(i, 1)
            if i + 1 < N_CHUNKS:
                stage1_exits_s(i + 1)
            if i + 2 == N_CHUNKS:
                for b in range(PACK):
                    nc.scalar.activation(
                        out=b1a[i + 1][:, b, :],
                        in_=b1bc[:],
                        func=ACT.Copy,
                        scale=attn[:, PACK * (i + 1) + b : PACK * (i + 1) + b + 1],
                    )
            for b in range(2, PACK):
                if i >= 1:
                    finish(i - 1, b)
                if i < N_CHUNKS:
                    stage2_mm(i, b)
            if i + 3 < N_CHUNKS:
                regroup_s(i + 3)
                regroup_v(i + 3)
            if i + 2 < N_CHUNKS:
                quant_inc(i + 2)
            if i + 1 < N_CHUNKS:
                stage1_exits_v(i + 1)
            if i + 2 < N_CHUNKS:
                stage1_mm(i + 2)
            if i < N_CHUNKS:
                finish(i, 0)
